import numpy as np
import ml_dtypes


def mxq(x, axis, fmt="e4m3"):
    dtype, down = {"e4m3": (ml_dtypes.float8_e4m3fn, 7), "e5m2": (ml_dtypes.float8_e5m2, 14)}[fmt]
    v = np.moveaxis(np.asarray(x, np.float32).astype(ml_dtypes.bfloat16).astype(np.float64), axis, -1)
    blocks = v.reshape(v.shape[:-1] + (-1, 32))
    amax = np.abs(blocks).max(-1, keepdims=True)
    byte = np.maximum(np.where(amax > 0, np.frexp(amax)[1] - 1 + 127, 0) - down, 1)
    scale = np.exp2(byte - 127.0)
    codes = (blocks / scale).astype(np.float32).astype(dtype).astype(np.float64)
    return np.moveaxis((codes * scale).reshape(v.shape), -1, axis)


WIDE = False


def mx_kscale(k):
    if not WIDE:
        return np.ones(k)
    levels = np.array([10, -10, 5, -5, 0])
    a = np.random.permutation(np.resize(levels, k // 512 * 4)).reshape(k // 512, 4)
    idx = np.arange(k)
    return np.exp2(a[idx // 512, idx % 128 // 32])


BF16 = ml_dtypes.bfloat16


def bf(x):
    return np.asarray(x, np.float32).astype(BF16)


def f64(x):
    return np.asarray(x).astype(np.float64)


B, Q, S, D = 4, 256, 512, 1024
EPS = 1e-8
SLOPE = 0.1
SMOOTH = 9.0


def l2norm(v, axis):
    return v / (np.sqrt(np.sum(v * v, axis=axis, keepdims=True) + EPS) + EPS)


def setup_inputs():
    s = mx_kscale(D)
    return {"query": bf(np.random.standard_normal((B, Q, D)) * 0.25 * s),
            "context": bf(np.random.standard_normal((B, S, D)) * 2.0 / s)}


def reference(query, context):
    q, c = f64(query), f64(context)
    attn = mxq(c, 2, "e4m3") @ mxq(q, 2, "e4m3").transpose(0, 2, 1)
    attn = np.where(attn >= 0.0, attn, SLOPE * attn)
    attn = l2norm(attn, 2)
    z = attn.transpose(0, 2, 1) * SMOOTH
    e = np.exp(z - z.max(2, keepdims=True))
    a = e / e.sum(2, keepdims=True)
    return mxq(a, 2, "e4m3") @ mxq(c, 1, "e4m3")

@@ -1,0 +1,273 @@
+from contextlib import ExitStack
+
+import concourse.mybir as mybir
+from concourse.masks import make_identity
+
+F32 = mybir.dt.float32
+BF16 = mybir.dt.bfloat16
+U32 = mybir.dt.uint32
+U8 = mybir.dt.uint8
+FP8X4 = mybir.dt.float8_e4m3fn_x4
+ACT = mybir.ActivationFunctionType
+ALU = mybir.AluOpType
+
+B, Q, S, D = 4, 256, 512, 1024
+EPS = 1e-8
+SLOPE = 0.1
+SMOOTH = 9.0
+
+P = 128
+PACK = 4
+K_PASS = P * PACK
+D_PASSES = D // K_PASS
+Q_TILES = Q // P
+S_TILES = S // P
+BANK = 512
+D_BANKS = D // BANK
+GROUP = 2 * P
+C_GROUPS = S // GROUP
+GROUP_WORDS = (GROUP // P) * (D // 2)
+
+FLOPS = 2 * 2 * B * S * Q * D
+
+
+def tile_smcmr_pa_kernel(tc, query, context, out):
+    nc = tc.nc
+    with ExitStack() as ctx:
+        const = ctx.enter_context(tc.tile_pool(name="const", bufs=1))
+        per_batch = ctx.enter_context(tc.tile_pool(name="per_batch", bufs=B))
+        per_group = ctx.enter_context(tc.tile_pool(name="per_group", bufs=B * (1 + C_GROUPS)))
+        per_half = ctx.enter_context(tc.tile_pool(name="per_half", bufs=B * D_BANKS))
+        stream = ctx.enter_context(tc.tile_pool(name="stream", bufs=4))
+        per_tile = ctx.enter_context(tc.tile_pool(name="per_tile", bufs=3 * Q_TILES))
+        psum = ctx.enter_context(tc.psum_pool(name="psum", bufs=8))
+
+        ident = const.tile([P, P], F32)
+        make_identity(nc, ident[:])
+        ones = const.tile([P, 2], F32)
+        nc.vector.memset(ones[:], 1.0)
+        half = const.tile([P, S_TILES], F32)
+        nc.vector.memset(half[:], 0.5)
+        minus_smooth = const.tile([P, 1], F32)
+        nc.vector.memset(minus_smooth[:], -SMOOTH)
+        first_exp = const.tile([P, 1], F32)
+        nc.scalar.activation(out=first_exp[:], in_=minus_smooth[:], func=ACT.Exp)
+
+        ctx.enter_context(tc.manual_schedule())
+
+        def in_range(b):
+            return 0 <= b < B
+
+        q_rows = []
+        c_rows = []
+        for b in range(B):
+            q_tile = per_batch.tile([P, Q_TILES * D], BF16)
+            nc.sync.dma_start(out=q_tile[:], in_=query[b].rearrange("(p j) d -> p (j d)", j=Q_TILES))
+            q_rows.append(q_tile)
+            c_tile = per_batch.tile([P, S_TILES * D], BF16)
+            c_dram = context[b].rearrange("(p t) d -> p (t d)", t=S_TILES)
+            for h in range(C_GROUPS):
+                part = slice(h * 2 * D, (h + 1) * 2 * D)
+                nc.sync.dma_start(out=c_tile[:, part], in_=c_dram[:, part])
+            c_rows.append(c_tile)
+
+        def quantise_along_features(words):
+            blocks = words.rearrange("p (r g u w) -> p r g u w", r=2, g=D_PASSES, u=2)
+            grouped = stream.tile([P, D_PASSES * GROUP * PACK], BF16, align_bytes=64)
+            grouped_words = grouped[:].bitcast(F32).rearrange(
+                "p (g r c u) -> p g r c u", g=D_PASSES, r=2, u=2
+            )
+            for g in range(D_PASSES):
+                planes = psum.tile([P, 2, 2, P], F32, tag="bank")
+                for r in range(2):
+                    for u in range(2):
+                        nc.tensor.transpose(planes[:, r, u, :], blocks[:, r, g, u, :], ident[:])
+                nc.scalar.copy(
+                    out=grouped_words[:, g], in_=planes[:].rearrange("p r u c -> p r c u")
+                )
+            codes = per_group.tile([P, D_PASSES * GROUP], U32, align_bytes=64)
+            scales = per_group.tile([P, D_PASSES * GROUP], U8, align_bytes=64)
+            nc.vector.quantize_mx(out=codes[:].bitcast(FP8X4), scales=scales[:], in_=grouped[:])
+            return codes, scales
+
+        def regroup_tokens(k):
+            source = c_rows[k // D_BANKS][:].rearrange(
+                "p (t n c i) -> p n c t i", t=S_TILES, n=D_BANKS, i=4
+            )
+            by_feature = stream.tile([P, BANK * PACK], BF16, align_bytes=64)
+            nc.vector.tensor_copy(
+                out=by_feature[:].rearrange("p (c i t) -> p c t i", i=4, t=S_TILES),
+                in_=source[:, k % D_BANKS],
+            )
+            return by_feature
+
+        def quantise_tokens(by_feature):
+            codes = per_half.tile([P, BANK], U32, align_bytes=64)
+            scales = per_half.tile([P, BANK], U8, align_bytes=64)
+            nc.vector.quantize_mx(out=codes[:].bitcast(FP8X4), scales=scales[:], in_=by_feature[:])
+            return codes, scales
+
+        def leaky_scores(b, h, leaky):
+            q_codes, q_scales = q_mx[b]
+            c_codes, c_scales = c_mx[b][h]
+            attn = psum.tile([P, 2, Q], F32, tag="bank")
+            for r in range(2):
+                for g in range(D_PASSES):
+                    tokens = slice(g * GROUP + r * P, g * GROUP + (r + 1) * P)
+                    queries = slice(g * GROUP, (g + 1) * GROUP)
+                    nc.tensor.matmul_mx(
+                        out=attn[:, r, :],
+                        lhsT=c_codes[:, tokens].bitcast(FP8X4),
+                        lhsT_scale=c_scales[:, tokens],
+                        rhs=q_codes[:, queries].bitcast(FP8X4),
+                        rhs_scale=q_scales[:, queries],
+                        start=(g == 0),
+                        stop=(g == D_PASSES - 1),
+                    )
+            tenth = per_half.tile([P, 2, Q], F32)
+            nc.scalar.mul(out=tenth[:], in_=attn[:], mul=SLOPE)
+            nc.vector.tensor_tensor(
+                out=leaky[:, 2 * h : 2 * h + 2, :], in0=attn[:], in1=tenth[:], op=ALU.max
+            )
+
+        def root_of_squares(leaky):
+            squares = stream.tile([P, Q], F32)
+            sum_squares = per_batch.tile([P, S_TILES], F32)
+            for t in range(S_TILES):
+                nc.scalar.activation(
+                    out=squares[:], in_=leaky[:, t, :], func=ACT.Square, accum_out=sum_squares[:, t : t + 1]
+                )
+            shifted = per_batch.tile([P, S_TILES], F32)
+            nc.gpsimd.tensor_scalar(
+                out=shifted[:], in0=sum_squares[:], scalar1=EPS, scalar2=1.0, op0=ALU.add, op1=ALU.mult
+            )
+            root = per_batch.tile([P, S_TILES], F32)
+            nc.gpsimd.tensor_tensor(out=root[:], in0=shifted[:], in1=half[:], op=ALU.pow)
+            return root
+
+        def gain_of(root):
+            norm_ninth = per_batch.tile([P, S_TILES], F32)
+            nc.vector.tensor_scalar(
+                out=norm_ninth[:], in0=root[:], scalar1=EPS, scalar2=1.0 / SMOOTH, op0=ALU.add, op1=ALU.mult
+            )
+            gain = per_batch.tile([P, S_TILES], F32)
+            nc.vector.reciprocal(out=gain[:], in_=norm_ninth[:])
+            return gain
+
+        def exponentials(leaky, gain):
+            expo = stream.tile([P, S_TILES, Q], F32)
+            for t in range(S_TILES):
+                nc.scalar.activation(
+                    out=expo[:, t, :],
+                    in_=leaky[:, t, :],
+                    func=ACT.Exp,
+                    scale=gain[:, t : t + 1],
+                    bias=minus_smooth[:],
+                )
+            return expo
+
+        def inverse_sums(expo):
+            made = []
+            for j in range(Q_TILES):
+                norm = psum.tile([P, BANK], F32, tag="bank")
+                for t in range(S_TILES):
+                    nc.tensor.matmul(
+                        out=norm[:, P : P + 2],
+                        lhsT=expo[:, t, j * P : (j + 1) * P],
+                        rhs=ones[:],
+                        start=(t == 0),
+                        stop=(t == S_TILES - 1),
+                    )
+                inverse = per_tile.tile([P, 1], F32)
+                nc.vector.reciprocal(out=inverse[:], in_=norm[:, P : P + 1])
+                made.append((norm, inverse))
+            return made
+
+        def quantised_weights(expo, norms):
+            for norm, inverse in norms:
+                nc.tensor.matmul(
+                    out=norm[:, 0:P], lhsT=inverse[:].to_broadcast([P, P]), rhs=ident[:], start=True, stop=True
+                )
+            made = []
+            for j in range(Q_TILES):
+                norm, inverse = norms[j]
+                weights = per_tile.tile([P, P, PACK], BF16, align_bytes=64)
+                nc.vector.tensor_tensor(
+                    out=weights[:],
+                    in0=expo[:, :, j * P : (j + 1) * P].rearrange("p t q -> p q t"),
+                    in1=norm[:, 0:P].unsqueeze(2).to_broadcast([P, P, PACK]),
+                    op=ALU.mult,
+                )
+                a_codes = per_tile.tile([P, P], U32, align_bytes=64)
+                a_scales = per_tile.tile([P, P], U8, align_bytes=64)
+                nc.vector.quantize_mx(
+                    out=a_codes[:].bitcast(FP8X4),
+                    scales=a_scales[:],
+                    in_=weights[:].rearrange("p q t -> p (q t)"),
+                )
+                made.append((a_codes, a_scales))
+            return made
+
+        def output(b, a_mx):
+            out_rows = out[b].rearrange("(p j) d -> p j d", j=Q_TILES)
+            for j in range(Q_TILES):
+                a_codes, a_scales = a_mx[j]
+                result = per_tile.tile([P, D], F32)
+                for n in range(D_BANKS):
+                    c_codes, c_scales = c_by_tokens[b * D_BANKS + n]
+                    acc = psum.tile([P, BANK], F32, tag="bank")
+                    nc.tensor.matmul_mx(
+                        out=acc[:],
+                        lhsT=a_codes[:].bitcast(FP8X4),
+                        lhsT_scale=a_scales[:],
+                        rhs=c_codes[:].bitcast(FP8X4),
+                        rhs_scale=c_scales[:],
+                        start=True,
+                        stop=True,
+                    )
+                    if j == Q_TILES - 1 and n == D_BANKS - 1:
+                        nc.vector.tensor_copy(out=result[:, n * BANK : (n + 1) * BANK], in_=acc[:])
+                    else:
+                        nc.scalar.copy(out=result[:, n * BANK : (n + 1) * BANK], in_=acc[:])
+                nc.sync.dma_start(out=out_rows[:, j, :], in_=result[:])
+
+        q_mx = []
+        c_mx = []
+        c_by_tokens = []
+        for b in range(B):
+            c_words = c_rows[b][:].bitcast(F32)
+            q_mx.append(quantise_along_features(q_rows[b][:].bitcast(F32)))
+            low = quantise_along_features(c_words[:, 0:GROUP_WORDS])
+            by_feature = regroup_tokens(b)
+            high = quantise_along_features(c_words[:, GROUP_WORDS : 2 * GROUP_WORDS])
+            c_by_tokens.append(quantise_tokens(by_feature))
+            c_mx.append((low, high))
+
+        leaky = []
+        for b in range(B):
+            leaky.append(per_batch.tile([P, S_TILES, Q], F32, name="leaky"))
+            for h in range(C_GROUPS):
+                leaky_scores(b, h, leaky[b])
+
+        root = {}
+        gain = {}
+        expo = {}
+        norms = {}
+        a_mx = {}
+        for i in range(B + 4):
+            if in_range(i - 1):
+                gain[i - 1] = gain_of(root[i - 1])
+            if in_range(i):
+                root[i] = root_of_squares(leaky[i])
+            if in_range(i - 2):
+                expo[i - 2] = exponentials(leaky[i - 2], gain[i - 2])
+            if in_range(i):
+                by_feature = regroup_tokens(B + i)
+            if in_range(i - 3):
+                a_mx[i - 3] = quantised_weights(expo[i - 3], norms[i - 3])
+            if in_range(i):
+                c_by_tokens.append(quantise_tokens(by_feature))
+            if in_range(i - 4):
+                output(i - 4, a_mx[i - 4])
+            if in_range(i - 2):
+                norms[i - 2] = inverse_sums(expo[i - 2])

@@ -10,6 +10,7 @@ U8 = mybir.dt.uint8
 FP8X4 = mybir.dt.float8_e4m3fn_x4
 ACT = mybir.ActivationFunctionType
 ALU = mybir.AluOpType
+AXIS = mybir.AxisListType
 
 B, Q, S, D = 4, 256, 512, 1024
 EPS = 1e-8
@@ -44,8 +45,6 @@ def tile_smcmr_pa_kernel(tc, query, context, out):
 
         ident = const.tile([P, P], F32)
         make_identity(nc, ident[:])
-        ones = const.tile([P, 2], F32)
-        nc.vector.memset(ones[:], 1.0)
         half = const.tile([P, S_TILES], F32)
         nc.vector.memset(half[:], 0.5)
         minus_smooth = const.tile([P, 1], F32)
@@ -172,22 +171,23 @@ def tile_smcmr_pa_kernel(tc, query, context, out):
                 norm = psum.tile([P, BANK], F32, tag="bank")
                 for t in range(S_TILES):
                     nc.tensor.matmul(
-                        out=norm[:, P : P + 2],
+                        out=norm[:, P : 2 * P],
                         lhsT=expo[:, t, j * P : (j + 1) * P],
-                        rhs=ones[:],
+                        rhs=ident[:],
+                        is_transpose=True,
                         start=(t == 0),
                         stop=(t == S_TILES - 1),
                     )
+                total = per_tile.tile([P, 1], F32)
+                nc.vector.tensor_reduce(out=total[:], in_=norm[:, P : 2 * P], axis=AXIS.X, op=ALU.add)
                 inverse = per_tile.tile([P, 1], F32)
-                nc.vector.reciprocal(out=inverse[:], in_=norm[:, P : P + 1])
+                nc.vector.reciprocal(out=inverse[:], in_=total[:])
                 made.append((norm, inverse))
             return made
 
         def quantised_weights(expo, norms):
             for norm, inverse in norms:
-                nc.tensor.matmul(
-                    out=norm[:, 0:P], lhsT=inverse[:].to_broadcast([P, P]), rhs=ident[:], start=True, stop=True
-                )
+                nc.tensor.transpose(norm[:, 0:P], inverse[:].to_broadcast([P, P]), ident[:])
             made = []
             for j in range(Q_TILES):
                 norm, inverse = norms[j]

@@ -40,7 +40,8 @@ def tile_smcmr_pa_kernel(tc, query, context, out):
         per_group = ctx.enter_context(tc.tile_pool(name="per_group", bufs=B * (1 + C_GROUPS)))
         per_half = ctx.enter_context(tc.tile_pool(name="per_half", bufs=B * D_BANKS))
         stream = ctx.enter_context(tc.tile_pool(name="stream", bufs=4))
-        per_tile = ctx.enter_context(tc.tile_pool(name="per_tile", bufs=3 * Q_TILES))
+        ahead = ctx.enter_context(tc.tile_pool(name="ahead", bufs=B * D_BANKS))
+        per_tile = ctx.enter_context(tc.tile_pool(name="per_tile", bufs=4))
         psum = ctx.enter_context(tc.psum_pool(name="psum", bufs=8))
 
         ident = const.tile([P, P], F32)
@@ -70,7 +71,7 @@ def tile_smcmr_pa_kernel(tc, query, context, out):
                 nc.sync.dma_start(out=c_tile[:, part], in_=c_dram[:, part])
             c_rows.append(c_tile)
 
-        def quantise_along_features(words):
+        def lay_features(words, shared):
             blocks = words.rearrange("p (r g u w) -> p r g u w", r=2, g=D_PASSES, u=2)
             grouped = stream.tile([P, D_PASSES * GROUP * PACK], BF16, align_bytes=64)
             grouped_words = grouped[:].bitcast(F32).rearrange(
@@ -81,9 +82,11 @@ def tile_smcmr_pa_kernel(tc, query, context, out):
                 for r in range(2):
                     for u in range(2):
                         nc.tensor.transpose(planes[:, r, u, :], blocks[:, r, g, u, :], ident[:])
-                nc.scalar.copy(
-                    out=grouped_words[:, g], in_=planes[:].rearrange("p r u c -> p r c u")
-                )
+                copy = nc.vector.tensor_copy if shared and g > 0 else nc.scalar.copy
+                copy(out=grouped_words[:, g], in_=planes[:].rearrange("p r u c -> p r c u"))
+            return grouped
+
+        def quantise_features(grouped):
             codes = per_group.tile([P, D_PASSES * GROUP], U32, align_bytes=64)
             scales = per_group.tile([P, D_PASSES * GROUP], U8, align_bytes=64)
             nc.vector.quantize_mx(out=codes[:].bitcast(FP8X4), scales=scales[:], in_=grouped[:])
@@ -93,7 +96,7 @@ def tile_smcmr_pa_kernel(tc, query, context, out):
             source = c_rows[k // D_BANKS][:].rearrange(
                 "p (t n c i) -> p n c t i", t=S_TILES, n=D_BANKS, i=4
             )
-            by_feature = stream.tile([P, BANK * PACK], BF16, align_bytes=64)
+            by_feature = ahead.tile([P, BANK * PACK], BF16, align_bytes=64)
             nc.vector.tensor_copy(
                 out=by_feature[:].rearrange("p (c i t) -> p c t i", i=4, t=S_TILES),
                 in_=source[:, k % D_BANKS],
@@ -123,16 +126,16 @@ def tile_smcmr_pa_kernel(tc, query, context, out):
                         start=(g == 0),
                         stop=(g == D_PASSES - 1),
                     )
-            tenth = per_half.tile([P, 2, Q], F32)
+            tenth = stream.tile([P, 2, Q], F32)
             nc.scalar.mul(out=tenth[:], in_=attn[:], mul=SLOPE)
             nc.vector.tensor_tensor(
                 out=leaky[:, 2 * h : 2 * h + 2, :], in0=attn[:], in1=tenth[:], op=ALU.max
             )
 
         def root_of_squares(leaky):
-            squares = stream.tile([P, Q], F32)
             sum_squares = per_batch.tile([P, S_TILES], F32)
             for t in range(S_TILES):
+                squares = stream.tile([P, Q], F32)
                 nc.scalar.activation(
                     out=squares[:], in_=leaky[:, t, :], func=ACT.Square, accum_out=sum_squares[:, t : t + 1]
                 )
@@ -144,14 +147,17 @@ def tile_smcmr_pa_kernel(tc, query, context, out):
             nc.gpsimd.tensor_tensor(out=root[:], in0=shifted[:], in1=half[:], op=ALU.pow)
             return root
 
-        def gain_of(root):
+        def ninth_of_norm(root):
             norm_ninth = per_batch.tile([P, S_TILES], F32)
             nc.vector.tensor_scalar(
                 out=norm_ninth[:], in0=root[:], scalar1=EPS, scalar2=1.0 / SMOOTH, op0=ALU.add, op1=ALU.mult
             )
-            gain = per_batch.tile([P, S_TILES], F32)
-            nc.vector.reciprocal(out=gain[:], in_=norm_ninth[:])
-            return gain
+            return norm_ninth
+
+        def inverted(values, width):
+            inverse = per_tile.tile([P, width], F32)
+            nc.vector.reciprocal(out=inverse[:], in_=values[:])
+            return inverse
 
         def exponentials(leaky, gain):
             expo = stream.tile([P, S_TILES, Q], F32)
@@ -165,109 +171,138 @@ def tile_smcmr_pa_kernel(tc, query, context, out):
                 )
             return expo
 
-        def inverse_sums(expo):
-            made = []
+        def partial_sums(expo):
+            norm = psum.tile([P, BANK], F32, tag="bank")
             for j in range(Q_TILES):
-                norm = psum.tile([P, BANK], F32, tag="bank")
                 for t in range(S_TILES):
                     nc.tensor.matmul(
-                        out=norm[:, P : 2 * P],
+                        out=norm[:, Q + j * P : Q + (j + 1) * P],
                         lhsT=expo[:, t, j * P : (j + 1) * P],
                         rhs=ident[:],
                         is_transpose=True,
                         start=(t == 0),
                         stop=(t == S_TILES - 1),
                     )
-                total = per_tile.tile([P, 1], F32)
-                nc.vector.tensor_reduce(out=total[:], in_=norm[:, P : 2 * P], axis=AXIS.X, op=ALU.add)
-                inverse = per_tile.tile([P, 1], F32)
-                nc.vector.reciprocal(out=inverse[:], in_=total[:])
-                made.append((norm, inverse))
-            return made
+            return norm
 
-        def quantised_weights(expo, norms):
-            for norm, inverse in norms:
-                nc.tensor.transpose(norm[:, 0:P], inverse[:].to_broadcast([P, P]), ident[:])
-            made = []
+        def sums_of(norm):
+            total = per_tile.tile([P, Q_TILES], F32)
+            nc.vector.tensor_reduce(
+                out=total[:],
+                in_=norm[:, Q : 2 * Q].rearrange("p (j m) -> p j m", j=Q_TILES),
+                axis=AXIS.X,
+                op=ALU.add,
+            )
+            return total
+
+        def normalised_weights(expo, norm, inverse):
             for j in range(Q_TILES):
-                norm, inverse = norms[j]
-                weights = per_tile.tile([P, P, PACK], BF16, align_bytes=64)
-                nc.vector.tensor_tensor(
-                    out=weights[:],
-                    in0=expo[:, :, j * P : (j + 1) * P].rearrange("p t q -> p q t"),
-                    in1=norm[:, 0:P].unsqueeze(2).to_broadcast([P, P, PACK]),
-                    op=ALU.mult,
+                nc.tensor.transpose(
+                    norm[:, j * P : (j + 1) * P], inverse[:, j : j + 1].to_broadcast([P, P]), ident[:]
                 )
-                a_codes = per_tile.tile([P, P], U32, align_bytes=64)
-                a_scales = per_tile.tile([P, P], U8, align_bytes=64)
-                nc.vector.quantize_mx(
-                    out=a_codes[:].bitcast(FP8X4),
-                    scales=a_scales[:],
-                    in_=weights[:].rearrange("p q t -> p (q t)"),
-                )
-                made.append((a_codes, a_scales))
-            return made
+            weights = per_tile.tile([P, Q, PACK], BF16, align_bytes=64)
+            nc.vector.tensor_tensor(
+                out=weights[:],
+                in0=expo[:].rearrange("p t q -> p q t"),
+                in1=norm[:, 0:Q].unsqueeze(2).to_broadcast([P, Q, PACK]),
+                op=ALU.mult,
+            )
+            return weights
+
+        def quantise_weights(weights):
+            a_codes = per_tile.tile([P, Q], U32, align_bytes=64)
+            a_scales = per_tile.tile([P, Q], U8, align_bytes=64)
+            nc.vector.quantize_mx(
+                out=a_codes[:].bitcast(FP8X4),
+                scales=a_scales[:],
+                in_=weights[:].rearrange("p q t -> p (q t)"),
+            )
+            return a_codes, a_scales
 
         def output(b, a_mx):
+            last = b == B - 1
             out_rows = out[b].rearrange("(p j) d -> p j d", j=Q_TILES)
+            a_codes, a_scales = a_mx
             for j in range(Q_TILES):
-                a_codes, a_scales = a_mx[j]
+                queries = slice(j * P, (j + 1) * P)
                 result = per_tile.tile([P, D], F32)
                 for n in range(D_BANKS):
                     c_codes, c_scales = c_by_tokens[b * D_BANKS + n]
                     acc = psum.tile([P, BANK], F32, tag="bank")
                     nc.tensor.matmul_mx(
                         out=acc[:],
-                        lhsT=a_codes[:].bitcast(FP8X4),
-                        lhsT_scale=a_scales[:],
+                        lhsT=a_codes[:, queries].bitcast(FP8X4),
+                        lhsT_scale=a_scales[:, queries],
                         rhs=c_codes[:].bitcast(FP8X4),
                         rhs_scale=c_scales[:],
                         start=True,
                         stop=True,
                     )
-                    if j == Q_TILES - 1 and n == D_BANKS - 1:
-                        nc.vector.tensor_copy(out=result[:, n * BANK : (n + 1) * BANK], in_=acc[:])
-                    else:
-                        nc.scalar.copy(out=result[:, n * BANK : (n + 1) * BANK], in_=acc[:])
-                nc.sync.dma_start(out=out_rows[:, j, :], in_=result[:])
+                    features = slice(n * BANK, (n + 1) * BANK)
+                    copy = nc.vector.tensor_copy if last and n > 0 else nc.scalar.copy
+                    copy(out=result[:, features], in_=acc[:])
+                    if last:
+                        nc.sync.dma_start(out=out_rows[:, j, features], in_=result[:, features])
+                if not last:
+                    nc.sync.dma_start(out=out_rows[:, j, :], in_=result[:])
 
+        by_feature = []
+        c_by_tokens = []
         q_mx = []
         c_mx = []
-        c_by_tokens = []
-        for b in range(B):
-            c_words = c_rows[b][:].bitcast(F32)
-            q_mx.append(quantise_along_features(q_rows[b][:].bitcast(F32)))
-            low = quantise_along_features(c_words[:, 0:GROUP_WORDS])
-            by_feature = regroup_tokens(b)
-            high = quantise_along_features(c_words[:, GROUP_WORDS : 2 * GROUP_WORDS])
-            c_by_tokens.append(quantise_tokens(by_feature))
-            c_mx.append((low, high))
-
         leaky = []
-        for b in range(B):
+
+        def regroup_next():
+            by_feature.append(regroup_tokens(len(by_feature)))
+
+        def quantise_next(count):
+            for k in range(count):
+                c_by_tokens.append(quantise_tokens(by_feature[len(c_by_tokens)]))
+
+        def scores(b):
             leaky.append(per_batch.tile([P, S_TILES, Q], F32, name="leaky"))
             for h in range(C_GROUPS):
                 leaky_scores(b, h, leaky[b])
 
+        for i in range(B):
+            c_words = c_rows[i][:].bitcast(F32)
+            of_q = lay_features(q_rows[i][:].bitcast(F32), i == 0)
+            of_low = lay_features(c_words[:, 0:GROUP_WORDS], False)
+            of_high = lay_features(c_words[:, GROUP_WORDS : 2 * GROUP_WORDS], False)
+            q_mx.append(quantise_features(of_q))
+            low_mx = quantise_features(of_low)
+            regroup_next()
+            c_mx.append((low_mx, quantise_features(of_high)))
+            if i % 2 == 0:
+                regroup_next()
+            if 0 < i < B - 1:
+                scores(i - 1)
+
         root = {}
-        gain = {}
         expo = {}
-        norms = {}
+        norm = {}
         a_mx = {}
-        for i in range(B + 4):
-            if in_range(i - 1):
-                gain[i - 1] = gain_of(root[i - 1])
+        for i in range(B + 3):
             if in_range(i):
                 root[i] = root_of_squares(leaky[i])
             if in_range(i - 2):
-                expo[i - 2] = exponentials(leaky[i - 2], gain[i - 2])
-            if in_range(i):
-                by_feature = regroup_tokens(B + i)
-            if in_range(i - 3):
-                a_mx[i - 3] = quantised_weights(expo[i - 3], norms[i - 3])
-            if in_range(i):
-                c_by_tokens.append(quantise_tokens(by_feature))
-            if in_range(i - 4):
-                output(i - 4, a_mx[i - 4])
+                total = sums_of(norm[i - 2])
+            if in_range(i - 1):
+                norm_ninth = ninth_of_norm(root[i - 1])
             if in_range(i - 2):
-                norms[i - 2] = inverse_sums(expo[i - 2])
+                inverse = inverted(total, Q_TILES)
+            if in_range(i - 1):
+                expo[i - 1] = exponentials(leaky[i - 1], inverted(norm_ninth, S_TILES))
+            if i in (1, 3):
+                regroup_next()
+            quantise_next((0, 2, 1, 0, 1, 1, 0)[i])
+            if in_range(i + 2):
+                scores(i + 2)
+            if in_range(i - 2):
+                weights = normalised_weights(expo[i - 2], norm[i - 2], inverse)
+                quantise_next((0, 0, 0, 1, 1, 1, 0)[i])
+                a_mx[i - 2] = quantise_weights(weights)
+            if in_range(i - 3):
+                output(i - 3, a_mx[i - 3])
+            if in_range(i - 1):
+                norm[i - 1] = partial_sums(expo[i - 1])

@@ -60,30 +60,34 @@ def tile_smcmr_pa_kernel(tc, query, context, out):
 
         q_rows = []
         c_rows = []
+        def load(tile, rows, row_tiles):
+            step = (1 if len(c_rows) == 0 else 2) * D
+            for start in range(0, row_tiles * D, step):
+                part = slice(start, start + step)
+                nc.sync.dma_start(out=tile[:, part], in_=rows[:, part])
+
         for b in range(B):
             q_tile = per_batch.tile([P, Q_TILES * D], BF16)
-            nc.sync.dma_start(out=q_tile[:], in_=query[b].rearrange("(p j) d -> p (j d)", j=Q_TILES))
+            load(q_tile, query[b].rearrange("(p j) d -> p (j d)", j=Q_TILES), Q_TILES)
             q_rows.append(q_tile)
             c_tile = per_batch.tile([P, S_TILES * D], BF16)
-            c_dram = context[b].rearrange("(p t) d -> p (t d)", t=S_TILES)
-            for h in range(C_GROUPS):
-                part = slice(h * 2 * D, (h + 1) * 2 * D)
-                nc.sync.dma_start(out=c_tile[:, part], in_=c_dram[:, part])
+            load(c_tile, context[b].rearrange("(p t) d -> p (t d)", t=S_TILES), S_TILES)
             c_rows.append(c_tile)
 
-        def lay_features(words, shared):
+        def lay_features(words):
             blocks = words.rearrange("p (r g u w) -> p r g u w", r=2, g=D_PASSES, u=2)
             grouped = stream.tile([P, D_PASSES * GROUP * PACK], BF16, align_bytes=64)
             grouped_words = grouped[:].bitcast(F32).rearrange(
                 "p (g r c u) -> p g r c u", g=D_PASSES, r=2, u=2
             )
-            for g in range(D_PASSES):
-                planes = psum.tile([P, 2, 2, P], F32, tag="bank")
-                for r in range(2):
+            for r in range(2):
+                planes = psum.tile([P, D_PASSES, 2, P], F32, tag="bank")
+                for g in range(D_PASSES):
                     for u in range(2):
-                        nc.tensor.transpose(planes[:, r, u, :], blocks[:, r, g, u, :], ident[:])
-                copy = nc.vector.tensor_copy if shared and g > 0 else nc.scalar.copy
-                copy(out=grouped_words[:, g], in_=planes[:].rearrange("p r u c -> p r c u"))
+                        nc.tensor.transpose(planes[:, g, u, :], blocks[:, r, g, u, :], ident[:])
+                nc.scalar.copy(
+                    out=grouped_words[:, :, r], in_=planes[:].rearrange("p g u c -> p g c u")
+                )
             return grouped
 
         def quantise_features(grouped):
@@ -266,9 +270,9 @@ def tile_smcmr_pa_kernel(tc, query, context, out):
 
         for i in range(B):
             c_words = c_rows[i][:].bitcast(F32)
-            of_q = lay_features(q_rows[i][:].bitcast(F32), i == 0)
-            of_low = lay_features(c_words[:, 0:GROUP_WORDS], False)
-            of_high = lay_features(c_words[:, GROUP_WORDS : 2 * GROUP_WORDS], False)
+            of_q = lay_features(q_rows[i][:].bitcast(F32))
+            of_low = lay_features(c_words[:, 0:GROUP_WORDS])
+            of_high = lay_features(c_words[:, GROUP_WORDS : 2 * GROUP_WORDS])
             q_mx.append(quantise_features(of_q))
             low_mx = quantise_features(of_low)
             regroup_next()

@@ -44,6 +44,9 @@ def tile_smcmr_pa_kernel(tc, query, context, out):
         per_tile = ctx.enter_context(tc.tile_pool(name="per_tile", bufs=4))
         psum = ctx.enter_context(tc.psum_pool(name="psum", bufs=8))
 
+        zeros = const.tile([P, Q], F32)
+        nc.vector.memset(zeros[:], 0.0)
+
         ident = const.tile([P, P], F32)
         make_identity(nc, ident[:])
         half = const.tile([P, S_TILES], F32)
@@ -250,6 +253,11 @@ def tile_smcmr_pa_kernel(tc, query, context, out):
                 if not last:
                     nc.sync.dma_start(out=out_rows[:, j, :], in_=result[:])
 
+        warm_up = psum.tile([P, BANK], F32, tag="bank")
+        for k in range(2):
+            nc.tensor.matmul(
+                out=warm_up[:, 0:Q], lhsT=zeros[:, 0:P], rhs=zeros[:], start=(k == 0), stop=(k == 1)
+            )
         by_feature = []
         c_by_tokens = []
         q_mx = []

@@ -58,6 +58,13 @@ def tile_smcmr_pa_kernel(tc, query, context, out):
 
         ctx.enter_context(tc.manual_schedule())
 
+        leaky = []
+        for b in range(B):
+            leaky.append(per_batch.tile([P, S_TILES, Q + 1], F32, name="leaky"))
+            nc.vector.tensor_scalar_mul(
+                out=leaky[b][:, :, Q : Q + 1], in0=half[:].unsqueeze(2), scalar1=2.0 * EPS**0.5
+            )
+
         def in_range(b):
             return 0 <= b < B
 
@@ -101,11 +108,11 @@ def tile_smcmr_pa_kernel(tc, query, context, out):
 
         def regroup_tokens(k):
             source = c_rows[k // D_BANKS][:].rearrange(
-                "p (t n c i) -> p n c t i", t=S_TILES, n=D_BANKS, i=4
+                "p (t n c i) -> p n c t i", t=S_TILES, n=D_BANKS, i=8
             )
             by_feature = ahead.tile([P, BANK * PACK], BF16, align_bytes=64)
             nc.vector.tensor_copy(
-                out=by_feature[:].rearrange("p (c i t) -> p c t i", i=4, t=S_TILES),
+                out=by_feature[:].rearrange("p (c i t) -> p c t i", i=8, t=S_TILES),
                 in_=source[:, k % D_BANKS],
             )
             return by_feature
@@ -136,22 +143,18 @@ def tile_smcmr_pa_kernel(tc, query, context, out):
             tenth = stream.tile([P, 2, Q], F32)
             nc.scalar.mul(out=tenth[:], in_=attn[:], mul=SLOPE)
             nc.vector.tensor_tensor(
-                out=leaky[:, 2 * h : 2 * h + 2, :], in0=attn[:], in1=tenth[:], op=ALU.max
+                out=leaky[:, 2 * h : 2 * h + 2, 0:Q], in0=attn[:], in1=tenth[:], op=ALU.max
             )
 
         def root_of_squares(leaky):
             sum_squares = per_batch.tile([P, S_TILES], F32)
             for t in range(S_TILES):
-                squares = stream.tile([P, Q], F32)
+                squares = stream.tile([P, Q + 1], F32)
                 nc.scalar.activation(
                     out=squares[:], in_=leaky[:, t, :], func=ACT.Square, accum_out=sum_squares[:, t : t + 1]
                 )
-            shifted = per_batch.tile([P, S_TILES], F32)
-            nc.gpsimd.tensor_scalar(
-                out=shifted[:], in0=sum_squares[:], scalar1=EPS, scalar2=1.0, op0=ALU.add, op1=ALU.mult
-            )
             root = per_batch.tile([P, S_TILES], F32)
-            nc.gpsimd.tensor_tensor(out=root[:], in0=shifted[:], in1=half[:], op=ALU.pow)
+            nc.gpsimd.tensor_tensor(out=root[:], in0=sum_squares[:], in1=half[:], op=ALU.pow)
             return root
 
         def ninth_of_norm(root):
@@ -171,7 +174,7 @@ def tile_smcmr_pa_kernel(tc, query, context, out):
             for t in range(S_TILES):
                 nc.scalar.activation(
                     out=expo[:, t, :],
-                    in_=leaky[:, t, :],
+                    in_=leaky[:, t, 0:Q],
                     func=ACT.Exp,
                     scale=gain[:, t : t + 1],
                     bias=minus_smooth[:],
@@ -227,6 +230,7 @@ def tile_smcmr_pa_kernel(tc, query, context, out):
             return a_codes, a_scales
 
         def output(b, a_mx):
+            fine = b >= B - 2
             last = b == B - 1
             out_rows = out[b].rearrange("(p j) d -> p j d", j=Q_TILES)
             a_codes, a_scales = a_mx
@@ -248,9 +252,9 @@ def tile_smcmr_pa_kernel(tc, query, context, out):
                     features = slice(n * BANK, (n + 1) * BANK)
                     copy = nc.vector.tensor_copy if last and n > 0 else nc.scalar.copy
                     copy(out=result[:, features], in_=acc[:])
-                    if last:
+                    if fine:
                         nc.sync.dma_start(out=out_rows[:, j, features], in_=result[:, features])
-                if not last:
+                if not fine:
                     nc.sync.dma_start(out=out_rows[:, j, :], in_=result[:])
 
         warm_up = psum.tile([P, BANK], F32, tag="bank")
@@ -262,7 +266,6 @@ def tile_smcmr_pa_kernel(tc, query, context, out):
         c_by_tokens = []
         q_mx = []
         c_mx = []
-        leaky = []
 
         def regroup_next():
             by_feature.append(regroup_tokens(len(by_feature)))
@@ -272,7 +275,6 @@ def tile_smcmr_pa_kernel(tc, query, context, out):
                 c_by_tokens.append(quantise_tokens(by_feature[len(c_by_tokens)]))
 
         def scores(b):
-            leaky.append(per_batch.tile([P, S_TILES, Q], F32, name="leaky"))
             for h in range(C_GROUPS):
                 leaky_scores(b, h, leaky[b])
 

@@ -59,8 +59,10 @@ def tile_smcmr_pa_kernel(tc, query, context, out):
         ctx.enter_context(tc.manual_schedule())
 
         leaky = []
+        square_sums = []
         for b in range(B):
             leaky.append(per_batch.tile([P, S_TILES, Q + 1], F32, name="leaky"))
+            square_sums.append(per_batch.tile([P, S_TILES], F32, name="square_sums"))
             nc.vector.tensor_scalar_mul(
                 out=leaky[b][:, :, Q : Q + 1], in0=half[:].unsqueeze(2), scalar1=2.0 * EPS**0.5
             )
@@ -71,7 +73,7 @@ def tile_smcmr_pa_kernel(tc, query, context, out):
         q_rows = []
         c_rows = []
         def load(tile, rows, row_tiles):
-            step = (1 if len(c_rows) == 0 else 2) * D
+            step = (1 if len(c_rows) < 2 else 2) * D
             for start in range(0, row_tiles * D, step):
                 part = slice(start, start + step)
                 nc.sync.dma_start(out=tile[:, part], in_=rows[:, part])
@@ -123,7 +125,7 @@ def tile_smcmr_pa_kernel(tc, query, context, out):
             nc.vector.quantize_mx(out=codes[:].bitcast(FP8X4), scales=scales[:], in_=by_feature[:])
             return codes, scales
 
-        def leaky_scores(b, h, leaky):
+        def multiply(b, h):
             q_codes, q_scales = q_mx[b]
             c_codes, c_scales = c_mx[b][h]
             attn = psum.tile([P, 2, Q], F32, tag="bank")
@@ -140,21 +142,28 @@ def tile_smcmr_pa_kernel(tc, query, context, out):
                         start=(g == 0),
                         stop=(g == D_PASSES - 1),
                     )
+            return attn
+
+        def tenth_of(attn):
             tenth = stream.tile([P, 2, Q], F32)
             nc.scalar.mul(out=tenth[:], in_=attn[:], mul=SLOPE)
+            return tenth
+
+        def maximum(b, h, attn, tenth):
             nc.vector.tensor_tensor(
-                out=leaky[:, 2 * h : 2 * h + 2, 0:Q], in0=attn[:], in1=tenth[:], op=ALU.max
+                out=leaky[b][:, 2 * h : 2 * h + 2, 0:Q], in0=attn[:], in1=tenth[:], op=ALU.max
             )
 
-        def root_of_squares(leaky):
-            sum_squares = per_batch.tile([P, S_TILES], F32)
-            for t in range(S_TILES):
+        def sum_squares(b, h):
+            for t in range(2 * h, 2 * h + 2):
                 squares = stream.tile([P, Q + 1], F32)
                 nc.scalar.activation(
-                    out=squares[:], in_=leaky[:, t, :], func=ACT.Square, accum_out=sum_squares[:, t : t + 1]
+                    out=squares[:], in_=leaky[b][:, t, :], func=ACT.Square, accum_out=square_sums[b][:, t : t + 1]
                 )
+
+        def root_of(square_sum):
             root = per_batch.tile([P, S_TILES], F32)
-            nc.gpsimd.tensor_tensor(out=root[:], in0=sum_squares[:], in1=half[:], op=ALU.pow)
+            nc.gpsimd.tensor_tensor(out=root[:], in0=square_sum[:], in1=half[:], op=ALU.pow)
             return root
 
         def ninth_of_norm(root):
@@ -205,11 +214,13 @@ def tile_smcmr_pa_kernel(tc, query, context, out):
             )
             return total
 
-        def normalised_weights(expo, norm, inverse):
+        def spread(norm, inverse):
             for j in range(Q_TILES):
                 nc.tensor.transpose(
                     norm[:, j * P : (j + 1) * P], inverse[:, j : j + 1].to_broadcast([P, P]), ident[:]
                 )
+
+        def normalised_weights(expo, norm):
             weights = per_tile.tile([P, Q, PACK], BF16, align_bytes=64)
             nc.vector.tensor_tensor(
                 out=weights[:],
@@ -230,13 +241,10 @@ def tile_smcmr_pa_kernel(tc, query, context, out):
             return a_codes, a_scales
 
         def output(b, a_mx):
-            fine = b >= B - 2
-            last = b == B - 1
-            out_rows = out[b].rearrange("(p j) d -> p j d", j=Q_TILES)
             a_codes, a_scales = a_mx
+            banks = []
             for j in range(Q_TILES):
                 queries = slice(j * P, (j + 1) * P)
-                result = per_tile.tile([P, D], F32)
                 for n in range(D_BANKS):
                     c_codes, c_scales = c_by_tokens[b * D_BANKS + n]
                     acc = psum.tile([P, BANK], F32, tag="bank")
@@ -249,6 +257,17 @@ def tile_smcmr_pa_kernel(tc, query, context, out):
                         start=True,
                         stop=True,
                     )
+                    banks.append(acc)
+            return banks
+
+        def store(b, banks):
+            fine = b >= B - 2
+            last = b == B - 1
+            out_rows = out[b].rearrange("(p j) d -> p j d", j=Q_TILES)
+            for j in range(Q_TILES):
+                result = per_tile.tile([P, D], F32)
+                for n in range(D_BANKS):
+                    acc = banks[j * D_BANKS + n]
                     features = slice(n * BANK, (n + 1) * BANK)
                     copy = nc.vector.tensor_copy if last and n > 0 else nc.scalar.copy
                     copy(out=result[:, features], in_=acc[:])
@@ -276,7 +295,8 @@ def tile_smcmr_pa_kernel(tc, query, context, out):
 
         def scores(b):
             for h in range(C_GROUPS):
-                leaky_scores(b, h, leaky[b])
+                attn = multiply(b, h)
+                maximum(b, h, attn, tenth_of(attn))
 
         for i in range(B):
             c_words = c_rows[i][:].bitcast(F32)
@@ -292,31 +312,71 @@ def tile_smcmr_pa_kernel(tc, query, context, out):
             if 0 < i < B - 1:
                 scores(i - 1)
 
-        root = {}
         expo = {}
         norm = {}
-        a_mx = {}
-        for i in range(B + 3):
-            if in_range(i):
-                root[i] = root_of_squares(leaky[i])
-            if in_range(i - 2):
-                total = sums_of(norm[i - 2])
-            if in_range(i - 1):
-                norm_ninth = ninth_of_norm(root[i - 1])
-            if in_range(i - 2):
-                inverse = inverted(total, Q_TILES)
-            if in_range(i - 1):
-                expo[i - 1] = exponentials(leaky[i - 1], inverted(norm_ninth, S_TILES))
-            if i in (1, 3):
+        norm_ninth = {}
+        gain = {}
+        total = {}
+        inverse = {}
+        root = {}
+        for h in range(C_GROUPS):
+            sum_squares(0, h)
+        root[0] = root_of(square_sums[0])
+        scores(2)
+        attn_low, attn_high = multiply(3, 0), multiply(3, 1)
+        norm_ninth[0] = ninth_of_norm(root[0])
+        gain[0] = inverted(norm_ninth[0], S_TILES)
+        quantise_next(1)
+        regroup_next()
+        sum_squares(1, 0)
+        tenth_low = tenth_of(attn_low)
+        expo[0] = exponentials(leaky[0], gain[0])
+        norm[0] = partial_sums(expo[0])
+        sum_squares(1, 1)
+        root[1] = root_of(square_sums[1])
+        tenth_high = tenth_of(attn_high)
+        total[0] = sums_of(norm[0])
+        maximum(3, 0, attn_low, tenth_low)
+        inverse[0] = inverted(total[0], Q_TILES)
+        maximum(3, 1, attn_high, tenth_high)
+        norm_ninth[1] = ninth_of_norm(root[1])
+        gain[1] = inverted(norm_ninth[1], S_TILES)
+        spread(norm[0], inverse[0])
+
+        for b in range(B):
+            if b + 2 < B:
+                for h in range(C_GROUPS):
+                    sum_squares(b + 2, h)
+                root[b + 2] = root_of(square_sums[b + 2])
+            if b + 1 < B:
+                expo[b + 1] = exponentials(leaky[b + 1], gain[b + 1])
+                norm[b + 1] = partial_sums(expo[b + 1])
+            if b > 0:
+                store(b - 1, banks)
+            weights = normalised_weights(expo[b], norm[b])
+            if b != 1:
+                quantise_next(1)
+            if b + 2 < B:
+                norm_ninth[b + 2] = ninth_of_norm(root[b + 2])
+            if 0 < b < B - 1:
+                total[b + 1] = sums_of(norm[b + 1])
+            if b == 1:
+                gain[b + 2] = inverted(norm_ninth[b + 2], S_TILES)
+            a_mx = quantise_weights(weights)
+            if b == 0:
+                quantise_next(1)
+                gain[b + 2] = inverted(norm_ninth[b + 2], S_TILES)
+                total[b + 1] = sums_of(norm[b + 1])
+            if b + 1 < B:
+                inverse[b + 1] = inverted(total[b + 1], Q_TILES)
+            if b == 0:
                 regroup_next()
-            quantise_next((0, 2, 1, 0, 1, 1, 0)[i])
-            if in_range(i + 2):
-                scores(i + 2)
-            if in_range(i - 2):
-                weights = normalised_weights(expo[i - 2], norm[i - 2], inverse)
-                quantise_next((0, 0, 0, 1, 1, 1, 0)[i])
-                a_mx[i - 2] = quantise_weights(weights)
-            if in_range(i - 3):
-                output(i - 3, a_mx[i - 3])
-            if in_range(i - 1):
-                norm[i - 1] = partial_sums(expo[i - 1])
+            if b > 0:
+                quantise_next(1)
+            if b == 0:
+                banks = output(b, a_mx)
+            if b + 1 < B:
+                spread(norm[b + 1], inverse[b + 1])
+            if b > 0:
+                banks = output(b, a_mx)
+        store(B - 1, banks)

@@ -110,11 +110,11 @@ def tile_smcmr_pa_kernel(tc, query, context, out):
 
         def regroup_tokens(k):
             source = c_rows[k // D_BANKS][:].rearrange(
-                "p (t n c i) -> p n c t i", t=S_TILES, n=D_BANKS, i=8
+                "p (t n c i) -> p n c t i", t=S_TILES, n=D_BANKS, i=2
             )
             by_feature = ahead.tile([P, BANK * PACK], BF16, align_bytes=64)
             nc.vector.tensor_copy(
-                out=by_feature[:].rearrange("p (c i t) -> p c t i", i=8, t=S_TILES),
+                out=by_feature[:].rearrange("p (c i t) -> p c t i", i=2, t=S_TILES),
                 in_=source[:, k % D_BANKS],
             )
             return by_feature

@@ -42,6 +42,7 @@ def tile_smcmr_pa_kernel(tc, query, context, out):
         stream = ctx.enter_context(tc.tile_pool(name="stream", bufs=4))
         ahead = ctx.enter_context(tc.tile_pool(name="ahead", bufs=B * D_BANKS))
         per_tile = ctx.enter_context(tc.tile_pool(name="per_tile", bufs=4))
+        results = ctx.enter_context(tc.tile_pool(name="results", bufs=B * Q_TILES))
         psum = ctx.enter_context(tc.psum_pool(name="psum", bufs=8))
 
         zeros = const.tile([P, Q], F32)
@@ -265,7 +266,7 @@ def tile_smcmr_pa_kernel(tc, query, context, out):
             last = b == B - 1
             out_rows = out[b].rearrange("(p j) d -> p j d", j=Q_TILES)
             for j in range(Q_TILES):
-                result = per_tile.tile([P, D], F32)
+                result = results.tile([P, D], F32)
                 for n in range(D_BANKS):
                     acc = banks[j * D_BANKS + n]
                     features = slice(n * BANK, (n + 1) * BANK)

from contextlib import ExitStack

import concourse.mybir as mybir
from concourse.masks import make_identity

F32 = mybir.dt.float32
BF16 = mybir.dt.bfloat16
U32 = mybir.dt.uint32
U8 = mybir.dt.uint8
FP8X4 = mybir.dt.float8_e4m3fn_x4
ACT = mybir.ActivationFunctionType
ALU = mybir.AluOpType
AXIS = mybir.AxisListType

B, Q, S, D = 4, 256, 512, 1024
EPS = 1e-8
SLOPE = 0.1
SMOOTH = 9.0

P = 128
PACK = 4
K_PASS = P * PACK
D_PASSES = D // K_PASS
Q_TILES = Q // P
S_TILES = S // P
BANK = 512
D_BANKS = D // BANK
GROUP = 2 * P
C_GROUPS = S // GROUP
GROUP_WORDS = (GROUP // P) * (D // 2)

FLOPS = 2 * 2 * B * S * Q * D


def tile_smcmr_pa_kernel(tc, query, context, out):
    nc = tc.nc
    with ExitStack() as ctx:
        const = ctx.enter_context(tc.tile_pool(name="const", bufs=1))
        per_batch = ctx.enter_context(tc.tile_pool(name="per_batch", bufs=B))
        per_group = ctx.enter_context(tc.tile_pool(name="per_group", bufs=B * (1 + C_GROUPS)))
        per_half = ctx.enter_context(tc.tile_pool(name="per_half", bufs=B * D_BANKS))
        stream = ctx.enter_context(tc.tile_pool(name="stream", bufs=4))
        ahead = ctx.enter_context(tc.tile_pool(name="ahead", bufs=B * D_BANKS))
        per_tile = ctx.enter_context(tc.tile_pool(name="per_tile", bufs=4))
        results = ctx.enter_context(tc.tile_pool(name="results", bufs=B * Q_TILES))
        psum = ctx.enter_context(tc.psum_pool(name="psum", bufs=8))

        zeros = const.tile([P, Q], F32)
        nc.vector.memset(zeros[:], 0.0)

        ident = const.tile([P, P], F32)
        make_identity(nc, ident[:])
        half = const.tile([P, S_TILES], F32)
        nc.vector.memset(half[:], 0.5)
        minus_smooth = const.tile([P, 1], F32)
        nc.vector.memset(minus_smooth[:], -SMOOTH)
        first_exp = const.tile([P, 1], F32)
        nc.scalar.activation(out=first_exp[:], in_=minus_smooth[:], func=ACT.Exp)

        ctx.enter_context(tc.manual_schedule())

        leaky = []
        square_sums = []
        for b in range(B):
            leaky.append(per_batch.tile([P, S_TILES, Q + 1], F32, name="leaky"))
            square_sums.append(per_batch.tile([P, S_TILES], F32, name="square_sums"))
            nc.vector.tensor_scalar_mul(
                out=leaky[b][:, :, Q : Q + 1], in0=half[:].unsqueeze(2), scalar1=2.0 * EPS**0.5
            )

        def in_range(b):
            return 0 <= b < B

        q_rows = []
        c_rows = []
        def load(tile, rows, row_tiles):
            step = (1 if len(c_rows) < 2 else 2) * D
            for start in range(0, row_tiles * D, step):
                part = slice(start, start + step)
                nc.sync.dma_start(out=tile[:, part], in_=rows[:, part])

        for b in range(B):
            q_tile = per_batch.tile([P, Q_TILES * D], BF16)
            load(q_tile, query[b].rearrange("(p j) d -> p (j d)", j=Q_TILES), Q_TILES)
            q_rows.append(q_tile)
            c_tile = per_batch.tile([P, S_TILES * D], BF16)
            load(c_tile, context[b].rearrange("(p t) d -> p (t d)", t=S_TILES), S_TILES)
            c_rows.append(c_tile)

        def lay_features(words):
            blocks = words.rearrange("p (r g u w) -> p r g u w", r=2, g=D_PASSES, u=2)
            grouped = stream.tile([P, D_PASSES * GROUP * PACK], BF16, align_bytes=64)
            grouped_words = grouped[:].bitcast(F32).rearrange(
                "p (g r c u) -> p g r c u", g=D_PASSES, r=2, u=2
            )
            for r in range(2):
                planes = psum.tile([P, D_PASSES, 2, P], F32, tag="bank")
                for g in range(D_PASSES):
                    for u in range(2):
                        nc.tensor.transpose(planes[:, g, u, :], blocks[:, r, g, u, :], ident[:])
                nc.scalar.copy(
                    out=grouped_words[:, :, r], in_=planes[:].rearrange("p g u c -> p g c u")
                )
            return grouped

        def quantise_features(grouped):
            codes = per_group.tile([P, D_PASSES * GROUP], U32, align_bytes=64)
            scales = per_group.tile([P, D_PASSES * GROUP], U8, align_bytes=64)
            nc.vector.quantize_mx(out=codes[:].bitcast(FP8X4), scales=scales[:], in_=grouped[:])
            return codes, scales

        def regroup_tokens(k):
            source = c_rows[k // D_BANKS][:].rearrange(
                "p (t n c i) -> p n c t i", t=S_TILES, n=D_BANKS, i=2
            )
            by_feature = ahead.tile([P, BANK * PACK], BF16, align_bytes=64)
            nc.vector.tensor_copy(
                out=by_feature[:].rearrange("p (c i t) -> p c t i", i=2, t=S_TILES),
                in_=source[:, k % D_BANKS],
            )
            return by_feature

        def quantise_tokens(by_feature):
            codes = per_half.tile([P, BANK], U32, align_bytes=64)
            scales = per_half.tile([P, BANK], U8, align_bytes=64)
            nc.vector.quantize_mx(out=codes[:].bitcast(FP8X4), scales=scales[:], in_=by_feature[:])
            return codes, scales

        def multiply(b, h):
            q_codes, q_scales = q_mx[b]
            c_codes, c_scales = c_mx[b][h]
            attn = psum.tile([P, 2, Q], F32, tag="bank")
            for r in range(2):
                for g in range(D_PASSES):
                    tokens = slice(g * GROUP + r * P, g * GROUP + (r + 1) * P)
                    queries = slice(g * GROUP, (g + 1) * GROUP)
                    nc.tensor.matmul_mx(
                        out=attn[:, r, :],
                        lhsT=c_codes[:, tokens].bitcast(FP8X4),
                        lhsT_scale=c_scales[:, tokens],
                        rhs=q_codes[:, queries].bitcast(FP8X4),
                        rhs_scale=q_scales[:, queries],
                        start=(g == 0),
                        stop=(g == D_PASSES - 1),
                    )
            return attn

        def tenth_of(attn):
            tenth = stream.tile([P, 2, Q], F32)
            nc.scalar.mul(out=tenth[:], in_=attn[:], mul=SLOPE)
            return tenth

        def maximum(b, h, attn, tenth):
            nc.vector.tensor_tensor(
                out=leaky[b][:, 2 * h : 2 * h + 2, 0:Q], in0=attn[:], in1=tenth[:], op=ALU.max
            )

        def sum_squares(b, h):
            for t in range(2 * h, 2 * h + 2):
                squares = stream.tile([P, Q + 1], F32)
                nc.scalar.activation(
                    out=squares[:], in_=leaky[b][:, t, :], func=ACT.Square, accum_out=square_sums[b][:, t : t + 1]
                )

        def root_of(square_sum):
            root = per_batch.tile([P, S_TILES], F32)
            nc.gpsimd.tensor_tensor(out=root[:], in0=square_sum[:], in1=half[:], op=ALU.pow)
            return root

        def ninth_of_norm(root):
            norm_ninth = per_batch.tile([P, S_TILES], F32)
            nc.vector.tensor_scalar(
                out=norm_ninth[:], in0=root[:], scalar1=EPS, scalar2=1.0 / SMOOTH, op0=ALU.add, op1=ALU.mult
            )
            return norm_ninth

        def inverted(values, width):
            inverse = per_tile.tile([P, width], F32)
            nc.vector.reciprocal(out=inverse[:], in_=values[:])
            return inverse

        def exponentials(leaky, gain):
            expo = stream.tile([P, S_TILES, Q], F32)
            for t in range(S_TILES):
                nc.scalar.activation(
                    out=expo[:, t, :],
                    in_=leaky[:, t, 0:Q],
                    func=ACT.Exp,
                    scale=gain[:, t : t + 1],
                    bias=minus_smooth[:],
                )
            return expo

        def partial_sums(expo):
            norm = psum.tile([P, BANK], F32, tag="bank")
            for j in range(Q_TILES):
                for t in range(S_TILES):
                    nc.tensor.matmul(
                        out=norm[:, Q + j * P : Q + (j + 1) * P],
                        lhsT=expo[:, t, j * P : (j + 1) * P],
                        rhs=ident[:],
                        is_transpose=True,
                        start=(t == 0),
                        stop=(t == S_TILES - 1),
                    )
            return norm

        def sums_of(norm):
            total = per_tile.tile([P, Q_TILES], F32)
            nc.vector.tensor_reduce(
                out=total[:],
                in_=norm[:, Q : 2 * Q].rearrange("p (j m) -> p j m", j=Q_TILES),
                axis=AXIS.X,
                op=ALU.add,
            )
            return total

        def spread(norm, inverse):
            for j in range(Q_TILES):
                nc.tensor.transpose(
                    norm[:, j * P : (j + 1) * P], inverse[:, j : j + 1].to_broadcast([P, P]), ident[:]
                )

        def normalised_weights(expo, norm):
            weights = per_tile.tile([P, Q, PACK], BF16, align_bytes=64)
            nc.vector.tensor_tensor(
                out=weights[:],
                in0=expo[:].rearrange("p t q -> p q t"),
                in1=norm[:, 0:Q].unsqueeze(2).to_broadcast([P, Q, PACK]),
                op=ALU.mult,
            )
            return weights

        def quantise_weights(weights):
            a_codes = per_tile.tile([P, Q], U32, align_bytes=64)
            a_scales = per_tile.tile([P, Q], U8, align_bytes=64)
            nc.vector.quantize_mx(
                out=a_codes[:].bitcast(FP8X4),
                scales=a_scales[:],
                in_=weights[:].rearrange("p q t -> p (q t)"),
            )
            return a_codes, a_scales

        def output(b, a_mx):
            a_codes, a_scales = a_mx
            banks = []
            for j in range(Q_TILES):
                queries = slice(j * P, (j + 1) * P)
                for n in range(D_BANKS):
                    c_codes, c_scales = c_by_tokens[b * D_BANKS + n]
                    acc = psum.tile([P, BANK], F32, tag="bank")
                    nc.tensor.matmul_mx(
                        out=acc[:],
                        lhsT=a_codes[:, queries].bitcast(FP8X4),
                        lhsT_scale=a_scales[:, queries],
                        rhs=c_codes[:].bitcast(FP8X4),
                        rhs_scale=c_scales[:],
                        start=True,
                        stop=True,
                    )
                    banks.append(acc)
            return banks

        def store(b, banks):
            fine = b >= B - 2
            last = b == B - 1
            out_rows = out[b].rearrange("(p j) d -> p j d", j=Q_TILES)
            for j in range(Q_TILES):
                result = results.tile([P, D], F32)
                for n in range(D_BANKS):
                    acc = banks[j * D_BANKS + n]
                    features = slice(n * BANK, (n + 1) * BANK)
                    copy = nc.vector.tensor_copy if last and n > 0 else nc.scalar.copy
                    copy(out=result[:, features], in_=acc[:])
                    if fine:
                        nc.sync.dma_start(out=out_rows[:, j, features], in_=result[:, features])
                if not fine:
                    nc.sync.dma_start(out=out_rows[:, j, :], in_=result[:])

        warm_up = psum.tile([P, BANK], F32, tag="bank")
        for k in range(2):
            nc.tensor.matmul(
                out=warm_up[:, 0:Q], lhsT=zeros[:, 0:P], rhs=zeros[:], start=(k == 0), stop=(k == 1)
            )
        by_feature = []
        c_by_tokens = []
        q_mx = []
        c_mx = []

        def regroup_next():
            by_feature.append(regroup_tokens(len(by_feature)))

        def quantise_next(count):
            for k in range(count):
                c_by_tokens.append(quantise_tokens(by_feature[len(c_by_tokens)]))

        def scores(b):
            for h in range(C_GROUPS):
                attn = multiply(b, h)
                maximum(b, h, attn, tenth_of(attn))

        for i in range(B):
            c_words = c_rows[i][:].bitcast(F32)
            of_q = lay_features(q_rows[i][:].bitcast(F32))
            of_low = lay_features(c_words[:, 0:GROUP_WORDS])
            of_high = lay_features(c_words[:, GROUP_WORDS : 2 * GROUP_WORDS])
            q_mx.append(quantise_features(of_q))
            low_mx = quantise_features(of_low)
            regroup_next()
            c_mx.append((low_mx, quantise_features(of_high)))
            if i % 2 == 0:
                regroup_next()
            if 0 < i < B - 1:
                scores(i - 1)

        expo = {}
        norm = {}
        norm_ninth = {}
        gain = {}
        total = {}
        inverse = {}
        root = {}
        for h in range(C_GROUPS):
            sum_squares(0, h)
        root[0] = root_of(square_sums[0])
        scores(2)
        attn_low, attn_high = multiply(3, 0), multiply(3, 1)
        norm_ninth[0] = ninth_of_norm(root[0])
        gain[0] = inverted(norm_ninth[0], S_TILES)
        quantise_next(1)
        regroup_next()
        sum_squares(1, 0)
        tenth_low = tenth_of(attn_low)
        expo[0] = exponentials(leaky[0], gain[0])
        norm[0] = partial_sums(expo[0])
        sum_squares(1, 1)
        root[1] = root_of(square_sums[1])
        tenth_high = tenth_of(attn_high)
        total[0] = sums_of(norm[0])
        maximum(3, 0, attn_low, tenth_low)
        inverse[0] = inverted(total[0], Q_TILES)
        maximum(3, 1, attn_high, tenth_high)
        norm_ninth[1] = ninth_of_norm(root[1])
        gain[1] = inverted(norm_ninth[1], S_TILES)
        spread(norm[0], inverse[0])

        for b in range(B):
            if b + 2 < B:
                for h in range(C_GROUPS):
                    sum_squares(b + 2, h)
                root[b + 2] = root_of(square_sums[b + 2])
            if b + 1 < B:
                expo[b + 1] = exponentials(leaky[b + 1], gain[b + 1])
                norm[b + 1] = partial_sums(expo[b + 1])
            if b > 0:
                store(b - 1, banks)
            weights = normalised_weights(expo[b], norm[b])
            if b != 1:
                quantise_next(1)
            if b + 2 < B:
                norm_ninth[b + 2] = ninth_of_norm(root[b + 2])
            if 0 < b < B - 1:
                total[b + 1] = sums_of(norm[b + 1])
            if b == 1:
                gain[b + 2] = inverted(norm_ninth[b + 2], S_TILES)
            a_mx = quantise_weights(weights)
            if b == 0:
                quantise_next(1)
                gain[b + 2] = inverted(norm_ninth[b + 2], S_TILES)
                total[b + 1] = sums_of(norm[b + 1])
            if b + 1 < B:
                inverse[b + 1] = inverted(total[b + 1], Q_TILES)
            if b == 0:
                regroup_next()
            if b > 0:
                quantise_next(1)
            if b == 0:
                banks = output(b, a_mx)
            if b + 1 < B:
                spread(norm[b + 1], inverse[b + 1])
            if b > 0:
                banks = output(b, a_mx)
        store(B - 1, banks)
